import numpy as np
import ml_dtypes


def mxq(x, axis, fmt="e4m3"):
    dtype, down = {"e4m3": (ml_dtypes.float8_e4m3fn, 7), "e5m2": (ml_dtypes.float8_e5m2, 14)}[fmt]
    v = np.moveaxis(np.asarray(x, np.float32).astype(ml_dtypes.bfloat16).astype(np.float64), axis, -1)
    blocks = v.reshape(v.shape[:-1] + (-1, 32))
    amax = np.abs(blocks).max(-1, keepdims=True)
    byte = np.maximum(np.where(amax > 0, np.frexp(amax)[1] - 1 + 127, 0) - down, 1)
    scale = np.exp2(byte - 127.0)
    codes = (blocks / scale).astype(np.float32).astype(dtype).astype(np.float64)
    return np.moveaxis((codes * scale).reshape(v.shape), -1, axis)


WIDE = False


def mx_kscale(k):
    if not WIDE:
        return np.ones(k)
    levels = np.array([10, -10, 5, -5, 0])
    a = np.random.permutation(np.resize(levels, k // 512 * 4)).reshape(k // 512, 4)
    idx = np.arange(k)
    return np.exp2(a[idx // 512, idx % 128 // 32])


BF16 = ml_dtypes.bfloat16


def bf(x):
    return np.asarray(x, np.float32).astype(BF16)


def f64(x):
    return np.asarray(x).astype(np.float64)


B, A, E, P, R = 1024, 8, 512, 512, 1024


def setup_inputs():
    s = mx_kscale(R)
    return {
        "attr_rep": bf(np.random.standard_normal((B, A, R)) * s),
        "bwd_proj": bf(np.random.standard_normal((A, R, P)) / np.sqrt(R) / s[:, None]),
        "self_weighted": bf(1.0 + 0.3 * np.random.standard_normal((1, A, 1))),
    }


def reference(attr_rep, bwd_proj, self_weighted):
    proj = (mxq(f64(attr_rep).transpose(1, 0, 2), 2, "e4m3") @ mxq(f64(bwd_proj), 1, "e4m3")).transpose(1, 0, 2)
    return np.sum(np.maximum(proj, 0.0) * f64(self_weighted), axis=1)

@@ -1,0 +1,217 @@
+from contextlib import ExitStack
+
+import concourse.mybir as mybir
+from concourse.masks import make_identity
+
+BF16 = mybir.dt.bfloat16
+F32 = mybir.dt.float32
+U32 = mybir.dt.uint32
+U8 = mybir.dt.uint8
+FP8X4 = mybir.dt.float8_e4m3fn_x4
+ALU = mybir.AluOpType
+ACT = mybir.ActivationFunctionType
+
+P = 128
+NODES, TYPES, K, N = 1024, 8, 1024, 512
+FLOPS = 2 * NODES * TYPES * K * N
+NODE_TILES = NODES // P
+PASSES = K // 512
+UNIT_TILES = 2
+UNITS_PER_TYPE = NODE_TILES // UNIT_TILES
+UNITS = TYPES * UNITS_PER_TYPE
+LEAD = 2
+AHEAD = 8
+
+
+def tile_attributegnn_pb_t_kernel(tc, attr_rep, bwd_proj, self_weighted, out):
+    nc = tc.nc
+    x_view = attr_rep.rearrange("(p m) a k -> p m a k", m=NODE_TILES)
+    w_view = bwd_proj.rearrange("a (g u q e) n -> a g q u e n", g=PASSES, u=2, q=P, e=2)
+    out_view = out.rearrange("(p m) n -> p m n", m=NODE_TILES)
+
+    with ExitStack() as ctx:
+        const = ctx.enter_context(tc.tile_pool(name="const", bufs=1))
+        xraw_pool = ctx.enter_context(tc.tile_pool(name="xraw", bufs=AHEAD + 4))
+        wraw_pool = ctx.enter_context(tc.tile_pool(name="wraw", bufs=8))
+        xgrp_pool = ctx.enter_context(tc.tile_pool(name="xgrp", bufs=3))
+        xq_pool = ctx.enter_context(tc.tile_pool(name="xq", bufs=3))
+        wgrp_pool = ctx.enter_context(tc.tile_pool(name="wgrp", bufs=2))
+        wq_pool = ctx.enter_context(tc.tile_pool(name="wq", bufs=4))
+        relu_pool = ctx.enter_context(tc.tile_pool(name="relu", bufs=3))
+        psum_t = ctx.enter_context(tc.psum_pool(name="psum_t", bufs=4))
+        psum_mm = ctx.enter_context(tc.psum_pool(name="psum_mm", bufs=4))
+        ctx.enter_context(tc.manual_schedule())
+
+        x_raw, x_t, x_grp, x_q = {}, {}, {}, {}
+        w_raw, w_grp, w_q = {}, {}, {}
+        proj, relu_out = {}, {}
+
+        ident = const.tile([P, P], F32, name="ident")
+        make_identity(nc, ident[:])
+        weight_bf = const.tile([P, TYPES], BF16, name="weight_bf")
+        nc.scalar.dma_start(
+            out=weight_bf[:], in_=self_weighted.rearrange("o a i -> (o a i)").partition_broadcast(P)
+        )
+        weight = const.tile([P, TYPES], F32, name="weight")
+        total = const.tile([P, NODE_TILES, N], F32, name="total")
+        warm_in = const.tile([P, 1], F32, name="warm_in")
+        warm_out = const.tile([P, 1], F32, name="warm_out")
+        nc.vector.memset(warm_in[:], 0.0)
+        nc.scalar.activation(out=warm_out[:], in_=warm_in[:], func=ACT.Relu)
+
+        def load_x(u):
+            a, quarter = divmod(u, UNITS_PER_TYPE)
+            raw = xraw_pool.tile([P, UNIT_TILES * K], BF16, name="x_raw")
+            nc.sync.dma_start(
+                out=raw[:].rearrange("p (m k) -> p m k", m=UNIT_TILES),
+                in_=x_view[:, UNIT_TILES * quarter : UNIT_TILES * (quarter + 1), a, :],
+            )
+            x_raw[u] = raw
+
+        def load_w(a, g):
+            raw = wraw_pool.tile([P, 4, N], BF16, name="w_raw")
+            nc.sync.dma_start(out=raw[:].rearrange("q (u e) n -> q u e n", u=2), in_=w_view[a, g])
+            w_raw[(a, g)] = raw
+
+        def transposes(u):
+            words = x_raw[u][:].bitcast(F32)
+            for m in range(UNIT_TILES):
+                bank = psum_t.tile([P, 4, P], F32, name="x_t")
+                for s in range(4):
+                    first = (4 * m + s) * P
+                    nc.tensor.transpose(bank[:, s, :], words[:, first : first + P], ident[:])
+                x_t[(u, m)] = bank
+
+        def evacuate(u):
+            grp = xgrp_pool.tile([P, UNIT_TILES * K], BF16, name="x_grp", align_bytes=64)
+            words = grp[:].bitcast(F32)
+            for m in range(UNIT_TILES):
+                nc.scalar.copy(
+                    out=words[:, 512 * m : 512 * (m + 1)].rearrange("p (g b u) -> p g b u", g=PASSES, u=2),
+                    in_=x_t[(u, m)][:].rearrange("p (g u) b -> p g b u", u=2),
+                )
+            x_grp[u] = grp
+
+        def quantise_x(u):
+            codes = xq_pool.tile([P, UNIT_TILES * PASSES * P], U32, name="x_codes", align_bytes=64)
+            scales = xq_pool.tile([P, UNIT_TILES * PASSES * P], U8, name="x_scales", align_bytes=64)
+            nc.vector.quantize_mx(out=codes[:].bitcast(FP8X4), scales=scales[:], in_=x_grp[u][:])
+            x_q[u] = (codes, scales)
+
+        def regroup_w(a, g):
+            grp = wgrp_pool.tile([P, N, 4], BF16, name="w_grp", align_bytes=64)
+            nc.vector.tensor_copy(
+                out=grp[:].rearrange("p (c i) t -> p c t i", i=4),
+                in_=w_raw[(a, g)][:].rearrange("p t (c i) -> p c t i", i=4),
+            )
+            w_grp[(a, g)] = grp
+
+        def quantise_w(a, g):
+            codes = wq_pool.tile([P, N], U32, name="w_codes", align_bytes=64)
+            scales = wq_pool.tile([P, N], U8, name="w_scales", align_bytes=64)
+            nc.vector.quantize_mx(
+                out=codes[:].bitcast(FP8X4), scales=scales[:], in_=w_grp[(a, g)][:].rearrange("p n t -> p (n t)")
+            )
+            w_q[(a, g)] = (codes, scales)
+
+        def multiply(u):
+            a = u // UNITS_PER_TYPE
+            codes, scales = x_q[u]
+            for m in range(UNIT_TILES):
+                acc = psum_mm.tile([P, N], F32, name="proj")
+                for g in range(PASSES):
+                    first = (PASSES * m + g) * P
+                    w_codes, w_scales = w_q[(a, g)]
+                    nc.tensor.matmul_mx(
+                        out=acc[:],
+                        lhsT=codes[:, first : first + P].bitcast(FP8X4),
+                        lhsT_scale=scales[:, first : first + P],
+                        rhs=w_codes[:].bitcast(FP8X4),
+                        rhs_scale=w_scales[:],
+                        start=(g == 0),
+                        stop=(g == PASSES - 1),
+                    )
+                proj[(u, m)] = acc
+
+        def relu(u):
+            r = relu_pool.tile([P, UNIT_TILES, N], F32, name="relu_out")
+            for m in range(UNIT_TILES):
+                nc.scalar.activation(out=r[:, m, :], in_=proj[(u, m)][:], func=ACT.Relu)
+            relu_out[u] = r
+
+        def accumulate(u):
+            a, quarter = divmod(u, UNITS_PER_TYPE)
+            rows = slice(UNIT_TILES * quarter, UNIT_TILES * (quarter + 1))
+            if a == 0:
+                nc.vector.tensor_scalar_mul(out=total[:, rows, :], in0=relu_out[u][:], scalar1=weight[:, 0:1])
+            else:
+                nc.vector.scalar_tensor_tensor(
+                    out=total[:, rows, :],
+                    in0=relu_out[u][:],
+                    scalar=weight[:, a : a + 1],
+                    in1=total[:, rows, :],
+                    op0=ALU.mult,
+                    op1=ALU.add,
+                )
+            if a == TYPES - 1:
+                nc.sync.dma_start(out=out_view[:, rows, :], in_=total[:, rows, :])
+
+        loads = [("x", 0), ("w", (0, 0)), ("x", 1), ("w", (0, 1)), ("x", 2), ("w", (1, 0)), ("x", 3), ("w", (1, 1))]
+        for a in range(1, TYPES):
+            loads.append(("x", 4 * a))
+            loads.append(("x", 4 * a + 1))
+            if a + 1 < TYPES:
+                loads.append(("w", (a + 1, 0)))
+            loads.append(("x", 4 * a + 2))
+            loads.append(("x", 4 * a + 3))
+            if a + 1 < TYPES:
+                loads.append(("w", (a + 1, 1)))
+        issued = [0]
+
+        def issue_loads(last_unit):
+            while issued[0] < len(loads):
+                kind, what = loads[issued[0]]
+                if kind == "x" and what > last_unit:
+                    break
+                if kind == "x":
+                    load_x(what)
+                else:
+                    load_w(what[0], what[1])
+                issued[0] += 1
+
+        w_steps = []
+        for a in range(1, TYPES):
+            for g in range(PASSES):
+                w_steps.append((regroup_w, a, g))
+                w_steps.append((quantise_w, a, g))
+
+        def w_step(j):
+            if 0 <= j < len(w_steps):
+                step, a, g = w_steps[j]
+                step(a, g)
+
+        issue_loads(LEAD + AHEAD - 1)
+        transposes(0)
+        evacuate(0)
+        transposes(1)
+        evacuate(1)
+        regroup_w(0, 0)
+        regroup_w(0, 1)
+        quantise_w(0, 0)
+        quantise_x(0)
+        quantise_w(0, 1)
+        nc.vector.tensor_copy(out=weight[:], in_=weight_bf[:])
+        w_step(0)
+        for i in range(UNITS):
+            issue_loads(i + LEAD + AHEAD)
+            if i + LEAD < UNITS:
+                transposes(i + LEAD)
+                evacuate(i + LEAD)
+            multiply(i)
+            relu(i)
+            if i + 1 < UNITS:
+                quantise_x(i + 1)
+            w_step(i + 1)
+            if i >= 1:
+                accumulate(i - 1)
+        accumulate(UNITS - 1)

@@ -21,6 +21,8 @@ UNITS_PER_TYPE = NODE_TILES // UNIT_TILES
 UNITS = TYPES * UNITS_PER_TYPE
 LEAD = 2
 AHEAD = 8
+SCALAR_COLS = 96
+SCALAR_COLS_HEAD = 160
 
 
 def tile_attributegnn_pb_t_kernel(tc, attr_rep, bwd_proj, self_weighted, out):
@@ -100,9 +102,14 @@ def tile_attributegnn_pb_t_kernel(tc, attr_rep, bwd_proj, self_weighted, out):
 
         def regroup_w(a, g):
             grp = wgrp_pool.tile([P, N, 4], BF16, name="w_grp", align_bytes=64)
+            cut = N - (SCALAR_COLS_HEAD if a == 0 else SCALAR_COLS)
             nc.vector.tensor_copy(
-                out=grp[:].rearrange("p (c i) t -> p c t i", i=4),
-                in_=w_raw[(a, g)][:].rearrange("p t (c i) -> p c t i", i=4),
+                out=grp[:, 0:cut, :].rearrange("p (c i) t -> p c t i", i=4),
+                in_=w_raw[(a, g)][:, :, 0:cut].rearrange("p t (c i) -> p c t i", i=4),
+            )
+            nc.scalar.copy(
+                out=grp[:, cut:N, :].rearrange("p (c i) t -> p c t i", i=4),
+                in_=w_raw[(a, g)][:, :, cut:N].rearrange("p t (c i) -> p c t i", i=4),
             )
             w_grp[(a, g)] = grp
 
@@ -134,29 +141,38 @@ def tile_attributegnn_pb_t_kernel(tc, attr_rep, bwd_proj, self_weighted, out):
                 proj[(u, m)] = acc
 
         def relu(u):
-            r = relu_pool.tile([P, UNIT_TILES, N], F32, name="relu_out")
+            if u % 2 == 0:
+                relu_out[u // 2] = relu_pool.tile([P, 2 * UNIT_TILES, N], F32, name="relu_out")
+            r = relu_out[u // 2]
             for m in range(UNIT_TILES):
-                nc.scalar.activation(out=r[:, m, :], in_=proj[(u, m)][:], func=ACT.Relu)
-            relu_out[u] = r
+                nc.scalar.activation(out=r[:, UNIT_TILES * (u % 2) + m, :], in_=proj[(u, m)][:], func=ACT.Relu)
 
-        def accumulate(u):
-            a, quarter = divmod(u, UNITS_PER_TYPE)
-            rows = slice(UNIT_TILES * quarter, UNIT_TILES * (quarter + 1))
+        def add_in(a, r, rows):
             if a == 0:
-                nc.vector.tensor_scalar_mul(out=total[:, rows, :], in0=relu_out[u][:], scalar1=weight[:, 0:1])
+                nc.vector.tensor_scalar_mul(out=total[:, rows, :], in0=r, scalar1=weight[:, 0:1])
             else:
                 nc.vector.scalar_tensor_tensor(
                     out=total[:, rows, :],
-                    in0=relu_out[u][:],
+                    in0=r,
                     scalar=weight[:, a : a + 1],
                     in1=total[:, rows, :],
                     op0=ALU.mult,
                     op1=ALU.add,
                 )
-            if a == TYPES - 1:
-                nc.sync.dma_start(out=out_view[:, rows, :], in_=total[:, rows, :])
 
-        loads = [("x", 0), ("w", (0, 0)), ("x", 1), ("w", (0, 1)), ("x", 2), ("w", (1, 0)), ("x", 3), ("w", (1, 1))]
+        def accumulate(u):
+            a, quarter = divmod(u, UNITS_PER_TYPE)
+            if a < TYPES - 1:
+                if u % 2 == 1:
+                    first = UNIT_TILES * (quarter - 1)
+                    add_in(a, relu_out[u // 2][:], slice(first, first + 2 * UNIT_TILES))
+            else:
+                for m in range(UNIT_TILES):
+                    row = UNIT_TILES * quarter + m
+                    add_in(a, relu_out[u // 2][:, UNIT_TILES * (u % 2) + m, :], row)
+                    nc.sync.dma_start(out=out_view[:, row, :], in_=total[:, row, :])
+
+        loads = [("w", (0, 0)), ("x", 0), ("w", (0, 1)), ("x", 1), ("w", (1, 0)), ("x", 2), ("x", 3), ("w", (1, 1))]
         for a in range(1, TYPES):
             loads.append(("x", 4 * a))
             loads.append(("x", 4 * a + 1))
@@ -191,13 +207,13 @@ def tile_attributegnn_pb_t_kernel(tc, attr_rep, bwd_proj, self_weighted, out):
                 step(a, g)
 
         issue_loads(LEAD + AHEAD - 1)
+        regroup_w(0, 0)
         transposes(0)
         evacuate(0)
+        quantise_w(0, 0)
+        regroup_w(0, 1)
         transposes(1)
         evacuate(1)
-        regroup_w(0, 0)
-        regroup_w(0, 1)
-        quantise_w(0, 0)
         quantise_x(0)
         quantise_w(0, 1)
         nc.vector.tensor_copy(out=weight[:], in_=weight_bf[:])

@@ -20,9 +20,9 @@ UNIT_TILES = 2
 UNITS_PER_TYPE = NODE_TILES // UNIT_TILES
 UNITS = TYPES * UNITS_PER_TYPE
 LEAD = 2
+SHORT_LEAD_UNITS = 3
 AHEAD = 8
-SCALAR_COLS = 96
-SCALAR_COLS_HEAD = 160
+SCALAR_COLS = (160, 0, 0, 64, 96, 96, 96, 64)
 
 
 def tile_attributegnn_pb_t_kernel(tc, attr_rep, bwd_proj, self_weighted, out):
@@ -102,15 +102,16 @@ def tile_attributegnn_pb_t_kernel(tc, attr_rep, bwd_proj, self_weighted, out):
 
         def regroup_w(a, g):
             grp = wgrp_pool.tile([P, N, 4], BF16, name="w_grp", align_bytes=64)
-            cut = N - (SCALAR_COLS_HEAD if a == 0 else SCALAR_COLS)
+            cut = N - SCALAR_COLS[a]
             nc.vector.tensor_copy(
                 out=grp[:, 0:cut, :].rearrange("p (c i) t -> p c t i", i=4),
                 in_=w_raw[(a, g)][:, :, 0:cut].rearrange("p t (c i) -> p c t i", i=4),
             )
-            nc.scalar.copy(
-                out=grp[:, cut:N, :].rearrange("p (c i) t -> p c t i", i=4),
-                in_=w_raw[(a, g)][:, :, cut:N].rearrange("p t (c i) -> p c t i", i=4),
-            )
+            if cut < N:
+                nc.scalar.copy(
+                    out=grp[:, cut:N, :].rearrange("p (c i) t -> p c t i", i=4),
+                    in_=w_raw[(a, g)][:, :, cut:N].rearrange("p t (c i) -> p c t i", i=4),
+                )
             w_grp[(a, g)] = grp
 
         def quantise_w(a, g):
@@ -212,22 +213,26 @@ def tile_attributegnn_pb_t_kernel(tc, attr_rep, bwd_proj, self_weighted, out):
         evacuate(0)
         quantise_w(0, 0)
         regroup_w(0, 1)
-        transposes(1)
-        evacuate(1)
         quantise_x(0)
         quantise_w(0, 1)
-        nc.vector.tensor_copy(out=weight[:], in_=weight_bf[:])
-        w_step(0)
+        transposed = 1
+        w_done = 0
         for i in range(UNITS):
             issue_loads(i + LEAD + AHEAD)
-            if i + LEAD < UNITS:
-                transposes(i + LEAD)
-                evacuate(i + LEAD)
+            lead = 1 if i < SHORT_LEAD_UNITS else LEAD
+            while transposed <= min(UNITS - 1, i + lead):
+                transposes(transposed)
+                evacuate(transposed)
+                transposed += 1
             multiply(i)
             relu(i)
             if i + 1 < UNITS:
                 quantise_x(i + 1)
-            w_step(i + 1)
+            if i == 0:
+                nc.vector.tensor_copy(out=weight[:], in_=weight_bf[:])
+            while w_done <= i + 1:
+                w_step(w_done)
+                w_done += 1
             if i >= 1:
                 accumulate(i - 1)
         accumulate(UNITS - 1)

@@ -22,7 +22,7 @@ UNITS = TYPES * UNITS_PER_TYPE
 LEAD = 2
 SHORT_LEAD_UNITS = 3
 AHEAD = 8
-SCALAR_COLS = (160, 0, 0, 64, 96, 96, 96, 64)
+SCALAR_COLS = (160, 0, 0, 0, 0, 64, 96, 64)
 
 
 def tile_attributegnn_pb_t_kernel(tc, attr_rep, bwd_proj, self_weighted, out):
@@ -41,7 +41,8 @@ def tile_attributegnn_pb_t_kernel(tc, attr_rep, bwd_proj, self_weighted, out):
         wq_pool = ctx.enter_context(tc.tile_pool(name="wq", bufs=4))
         relu_pool = ctx.enter_context(tc.tile_pool(name="relu", bufs=3))
         psum_t = ctx.enter_context(tc.psum_pool(name="psum_t", bufs=4))
-        psum_mm = ctx.enter_context(tc.psum_pool(name="psum_mm", bufs=4))
+        psum_mm = ctx.enter_context(tc.psum_pool(name="psum_mm", bufs=3))
+        psum_sum = ctx.enter_context(tc.psum_pool(name="psum_sum", bufs=1))
         ctx.enter_context(tc.manual_schedule())
 
         x_raw, x_t, x_grp, x_q = {}, {}, {}, {}
@@ -55,6 +56,13 @@ def tile_attributegnn_pb_t_kernel(tc, attr_rep, bwd_proj, self_weighted, out):
             out=weight_bf[:], in_=self_weighted.rearrange("o a i -> (o a i)").partition_broadcast(P)
         )
         weight = const.tile([P, TYPES], F32, name="weight")
+        nc.gpsimd.tensor_copy(out=weight[:], in_=weight_bf[:])
+        diag = const.tile([P, TYPES, P], F32, name="diag")
+        for a in range(TYPES):
+            nc.gpsimd.tensor_scalar(
+                out=diag[:, a, :], in0=ident[:], scalar1=weight[:, a : a + 1], scalar2=0.0, op0=ALU.mult, op1=ALU.add
+            )
+        tile0_sum = psum_sum.tile([P, N], F32, name="tile0_sum")
         total = const.tile([P, NODE_TILES, N], F32, name="total")
         warm_in = const.tile([P, 1], F32, name="warm_in")
         warm_out = const.tile([P, 1], F32, name="warm_out")
@@ -161,15 +169,30 @@ def tile_attributegnn_pb_t_kernel(tc, attr_rep, bwd_proj, self_weighted, out):
                     op1=ALU.add,
                 )
 
+        def accumulate_tile0(a):
+            nc.tensor.matmul(
+                out=tile0_sum[:],
+                lhsT=diag[:, a, :],
+                rhs=relu_out[2 * a][:, 0, :],
+                start=(a == 0),
+                stop=(a == TYPES - 1),
+            )
+            if a == TYPES - 1:
+                nc.scalar.copy(out=total[:, 0, :], in_=tile0_sum[:])
+                nc.sync.dma_start(out=out_view[:, 0, :], in_=total[:, 0, :])
+
         def accumulate(u):
             a, quarter = divmod(u, UNITS_PER_TYPE)
             if a < TYPES - 1:
                 if u % 2 == 1:
+                    skip = 1 if quarter == 1 else 0
                     first = UNIT_TILES * (quarter - 1)
-                    add_in(a, relu_out[u // 2][:], slice(first, first + 2 * UNIT_TILES))
+                    add_in(a, relu_out[u // 2][:, skip : 2 * UNIT_TILES, :], slice(first + skip, first + 2 * UNIT_TILES))
             else:
                 for m in range(UNIT_TILES):
                     row = UNIT_TILES * quarter + m
+                    if row == 0:
+                        continue
                     add_in(a, relu_out[u // 2][:, UNIT_TILES * (u % 2) + m, :], row)
                     nc.sync.dma_start(out=out_view[:, row, :], in_=total[:, row, :])
 
@@ -226,10 +249,10 @@ def tile_attributegnn_pb_t_kernel(tc, attr_rep, bwd_proj, self_weighted, out):
                 transposed += 1
             multiply(i)
             relu(i)
+            if i % UNITS_PER_TYPE == 1:
+                accumulate_tile0(i // UNITS_PER_TYPE)
             if i + 1 < UNITS:
                 quantise_x(i + 1)
-            if i == 0:
-                nc.vector.tensor_copy(out=weight[:], in_=weight_bf[:])
             while w_done <= i + 1:
                 w_step(w_done)
                 w_done += 1

@@ -156,7 +156,7 @@ def tile_attributegnn_pb_t_kernel(tc, attr_rep, bwd_proj, self_weighted, out):
             for m in range(UNIT_TILES):
                 nc.scalar.activation(out=r[:, UNIT_TILES * (u % 2) + m, :], in_=proj[(u, m)][:], func=ACT.Relu)
 
-        def add_in(a, r, rows):
+        def add_in(a, r, rows, so_far=None):
             if a == 0:
                 nc.vector.tensor_scalar_mul(out=total[:, rows, :], in0=r, scalar1=weight[:, 0:1])
             else:
@@ -164,7 +164,7 @@ def tile_attributegnn_pb_t_kernel(tc, attr_rep, bwd_proj, self_weighted, out):
                     out=total[:, rows, :],
                     in0=r,
                     scalar=weight[:, a : a + 1],
-                    in1=total[:, rows, :],
+                    in1=total[:, rows, :] if so_far is None else so_far,
                     op0=ALU.mult,
                     op1=ALU.add,
                 )
@@ -175,11 +175,8 @@ def tile_attributegnn_pb_t_kernel(tc, attr_rep, bwd_proj, self_weighted, out):
                 lhsT=diag[:, a, :],
                 rhs=relu_out[2 * a][:, 0, :],
                 start=(a == 0),
-                stop=(a == TYPES - 1),
+                stop=(a == TYPES - 2),
             )
-            if a == TYPES - 1:
-                nc.scalar.copy(out=total[:, 0, :], in_=tile0_sum[:])
-                nc.sync.dma_start(out=out_view[:, 0, :], in_=total[:, 0, :])
 
         def accumulate(u):
             a, quarter = divmod(u, UNITS_PER_TYPE)
@@ -191,9 +188,7 @@ def tile_attributegnn_pb_t_kernel(tc, attr_rep, bwd_proj, self_weighted, out):
             else:
                 for m in range(UNIT_TILES):
                     row = UNIT_TILES * quarter + m
-                    if row == 0:
-                        continue
-                    add_in(a, relu_out[u // 2][:, UNIT_TILES * (u % 2) + m, :], row)
+                    add_in(a, relu_out[u // 2][:, UNIT_TILES * (u % 2) + m, :], row, tile0_sum[:] if row == 0 else None)
                     nc.sync.dma_start(out=out_view[:, row, :], in_=total[:, row, :])
 
         loads = [("w", (0, 0)), ("x", 0), ("w", (0, 1)), ("x", 1), ("w", (1, 0)), ("x", 2), ("x", 3), ("w", (1, 1))]
@@ -249,7 +244,7 @@ def tile_attributegnn_pb_t_kernel(tc, attr_rep, bwd_proj, self_weighted, out):
                 transposed += 1
             multiply(i)
             relu(i)
-            if i % UNITS_PER_TYPE == 1:
+            if i % UNITS_PER_TYPE == 1 and i // UNITS_PER_TYPE < TYPES - 1:
                 accumulate_tile0(i // UNITS_PER_TYPE)
             if i + 1 < UNITS:
                 quantise_x(i + 1)

@@ -14,11 +14,14 @@ ACT = mybir.ActivationFunctionType
 P = 128
 NODES, TYPES, K, N = 1024, 8, 1024, 512
 FLOPS = 2 * NODES * TYPES * K * N
+PACK = 4
+PASSES = K // (P * PACK)
 NODE_TILES = NODES // P
-PASSES = K // 512
 UNIT_TILES = 2
 UNITS_PER_TYPE = NODE_TILES // UNIT_TILES
 UNITS = TYPES * UNITS_PER_TYPE
+WORDS = K // 2
+
 LEAD = 2
 SHORT_LEAD_UNITS = 3
 AHEAD = 8
@@ -27,20 +30,20 @@ SCALAR_COLS = (160, 0, 0, 0, 0, 64, 96, 64)
 
 def tile_attributegnn_pb_t_kernel(tc, attr_rep, bwd_proj, self_weighted, out):
     nc = tc.nc
-    x_view = attr_rep.rearrange("(p m) a k -> p m a k", m=NODE_TILES)
-    w_view = bwd_proj.rearrange("a (g u q e) n -> a g q u e n", g=PASSES, u=2, q=P, e=2)
-    out_view = out.rearrange("(p m) n -> p m n", m=NODE_TILES)
+    x_view = attr_rep.rearrange("(r m) a k -> r m a k", m=NODE_TILES)
+    w_view = bwd_proj.rearrange("a (g h q e) n -> a g q h e n", g=PASSES, h=2, q=P, e=2)
+    out_view = out.rearrange("(r m) n -> r m n", m=NODE_TILES)
 
     with ExitStack() as ctx:
         const = ctx.enter_context(tc.tile_pool(name="const", bufs=1))
-        xraw_pool = ctx.enter_context(tc.tile_pool(name="xraw", bufs=AHEAD + 4))
+        xraw_pool = ctx.enter_context(tc.tile_pool(name="xraw", bufs=LEAD + AHEAD + 2))
         wraw_pool = ctx.enter_context(tc.tile_pool(name="wraw", bufs=8))
         xgrp_pool = ctx.enter_context(tc.tile_pool(name="xgrp", bufs=3))
         xq_pool = ctx.enter_context(tc.tile_pool(name="xq", bufs=3))
         wgrp_pool = ctx.enter_context(tc.tile_pool(name="wgrp", bufs=2))
-        wq_pool = ctx.enter_context(tc.tile_pool(name="wq", bufs=4))
+        wq_pool = ctx.enter_context(tc.tile_pool(name="wq", bufs=2 * PASSES))
         relu_pool = ctx.enter_context(tc.tile_pool(name="relu", bufs=3))
-        psum_t = ctx.enter_context(tc.psum_pool(name="psum_t", bufs=4))
+        psum_t = ctx.enter_context(tc.psum_pool(name="psum_t", bufs=2 * UNIT_TILES))
         psum_mm = ctx.enter_context(tc.psum_pool(name="psum_mm", bufs=3))
         psum_sum = ctx.enter_context(tc.psum_pool(name="psum_sum", bufs=1))
         ctx.enter_context(tc.manual_schedule())
@@ -51,16 +54,16 @@ def tile_attributegnn_pb_t_kernel(tc, attr_rep, bwd_proj, self_weighted, out):
 
         ident = const.tile([P, P], F32, name="ident")
         make_identity(nc, ident[:])
-        weight_bf = const.tile([P, TYPES], BF16, name="weight_bf")
+        gain_bf = const.tile([P, TYPES], BF16, name="gain_bf")
         nc.scalar.dma_start(
-            out=weight_bf[:], in_=self_weighted.rearrange("o a i -> (o a i)").partition_broadcast(P)
+            out=gain_bf[:], in_=self_weighted.rearrange("o a i -> (o a i)").partition_broadcast(P)
         )
-        weight = const.tile([P, TYPES], F32, name="weight")
-        nc.gpsimd.tensor_copy(out=weight[:], in_=weight_bf[:])
-        diag = const.tile([P, TYPES, P], F32, name="diag")
-        for a in range(TYPES):
+        gain = const.tile([P, TYPES], F32, name="gain")
+        nc.gpsimd.tensor_copy(out=gain[:], in_=gain_bf[:])
+        diag = const.tile([P, TYPES - 1, P], F32, name="diag")
+        for a in range(TYPES - 1):
             nc.gpsimd.tensor_scalar(
-                out=diag[:, a, :], in0=ident[:], scalar1=weight[:, a : a + 1], scalar2=0.0, op0=ALU.mult, op1=ALU.add
+                out=diag[:, a, :], in0=ident[:], scalar1=gain[:, a : a + 1], scalar2=0.0, op0=ALU.mult, op1=ALU.add
             )
         tile0_sum = psum_sum.tile([P, N], F32, name="tile0_sum")
         total = const.tile([P, NODE_TILES, N], F32, name="total")
@@ -69,36 +72,40 @@ def tile_attributegnn_pb_t_kernel(tc, attr_rep, bwd_proj, self_weighted, out):
         nc.vector.memset(warm_in[:], 0.0)
         nc.scalar.activation(out=warm_out[:], in_=warm_in[:], func=ACT.Relu)
 
-        def load_x(u):
+        def load_w(a, g):
+            raw = wraw_pool.tile([P, PACK, N], BF16, name="w_raw")
+            nc.sync.dma_start(out=raw[:].rearrange("q (h e) n -> q h e n", h=2), in_=w_view[a, g])
+            w_raw[(a, g)] = raw
+
+        def load_unit(u):
             a, quarter = divmod(u, UNITS_PER_TYPE)
             raw = xraw_pool.tile([P, UNIT_TILES * K], BF16, name="x_raw")
             nc.sync.dma_start(
-                out=raw[:].rearrange("p (m k) -> p m k", m=UNIT_TILES),
+                out=raw[:].rearrange("p (v k) -> p v k", v=UNIT_TILES),
                 in_=x_view[:, UNIT_TILES * quarter : UNIT_TILES * (quarter + 1), a, :],
             )
             x_raw[u] = raw
-
-        def load_w(a, g):
-            raw = wraw_pool.tile([P, 4, N], BF16, name="w_raw")
-            nc.sync.dma_start(out=raw[:].rearrange("q (u e) n -> q u e n", u=2), in_=w_view[a, g])
-            w_raw[(a, g)] = raw
+            if u == 0:
+                load_w(0, 1)
+            elif u % 2 == 1 and (u + 3) // UNITS_PER_TYPE < TYPES:
+                load_w((u + 3) // UNITS_PER_TYPE, ((u + 3) % UNITS_PER_TYPE) // 2)
 
         def transposes(u):
             words = x_raw[u][:].bitcast(F32)
-            for m in range(UNIT_TILES):
-                bank = psum_t.tile([P, 4, P], F32, name="x_t")
-                for s in range(4):
-                    first = (4 * m + s) * P
+            for v in range(UNIT_TILES):
+                bank = psum_t.tile([P, 2 * PASSES, P], F32, name="x_t")
+                for s in range(2 * PASSES):
+                    first = v * WORDS + s * P
                     nc.tensor.transpose(bank[:, s, :], words[:, first : first + P], ident[:])
-                x_t[(u, m)] = bank
+                x_t[(u, v)] = bank
 
         def evacuate(u):
             grp = xgrp_pool.tile([P, UNIT_TILES * K], BF16, name="x_grp", align_bytes=64)
             words = grp[:].bitcast(F32)
-            for m in range(UNIT_TILES):
+            for v in range(UNIT_TILES):
                 nc.scalar.copy(
-                    out=words[:, 512 * m : 512 * (m + 1)].rearrange("p (g b u) -> p g b u", g=PASSES, u=2),
-                    in_=x_t[(u, m)][:].rearrange("p (g u) b -> p g b u", u=2),
+                    out=words[:, v * WORDS : (v + 1) * WORDS].rearrange("p (g r h) -> p g r h", g=PASSES, h=2),
+                    in_=x_t[(u, v)][:].rearrange("p (g h) r -> p g r h", h=2),
                 )
             x_grp[u] = grp
 
@@ -109,16 +116,16 @@ def tile_attributegnn_pb_t_kernel(tc, attr_rep, bwd_proj, self_weighted, out):
             x_q[u] = (codes, scales)
 
         def regroup_w(a, g):
-            grp = wgrp_pool.tile([P, N, 4], BF16, name="w_grp", align_bytes=64)
+            grp = wgrp_pool.tile([P, N, PACK], BF16, name="w_grp", align_bytes=64)
             cut = N - SCALAR_COLS[a]
             nc.vector.tensor_copy(
-                out=grp[:, 0:cut, :].rearrange("p (c i) t -> p c t i", i=4),
-                in_=w_raw[(a, g)][:, :, 0:cut].rearrange("p t (c i) -> p c t i", i=4),
+                out=grp[:, 0:cut, :].rearrange("p (c d) t -> p c t d", d=4),
+                in_=w_raw[(a, g)][:, :, 0:cut].rearrange("p t (c d) -> p c t d", d=4),
             )
             if cut < N:
                 nc.scalar.copy(
-                    out=grp[:, cut:N, :].rearrange("p (c i) t -> p c t i", i=4),
-                    in_=w_raw[(a, g)][:, :, cut:N].rearrange("p t (c i) -> p c t i", i=4),
+                    out=grp[:, cut:N, :].rearrange("p (c d) t -> p c t d", d=4),
+                    in_=w_raw[(a, g)][:, :, cut:N].rearrange("p t (c d) -> p c t d", d=4),
                 )
             w_grp[(a, g)] = grp
 
@@ -130,16 +137,24 @@ def tile_attributegnn_pb_t_kernel(tc, attr_rep, bwd_proj, self_weighted, out):
             )
             w_q[(a, g)] = (codes, scales)
 
+        def weight_step(step):
+            a, g = 1 + step // (2 * PASSES), (step // 2) % PASSES
+            if a < TYPES:
+                if step % 2 == 0:
+                    regroup_w(a, g)
+                else:
+                    quantise_w(a, g)
+
         def multiply(u):
             a = u // UNITS_PER_TYPE
             codes, scales = x_q[u]
-            for m in range(UNIT_TILES):
-                acc = psum_mm.tile([P, N], F32, name="proj")
+            for v in range(UNIT_TILES):
+                product = psum_mm.tile([P, N], F32, name="proj")
                 for g in range(PASSES):
-                    first = (PASSES * m + g) * P
+                    first = (PASSES * v + g) * P
                     w_codes, w_scales = w_q[(a, g)]
                     nc.tensor.matmul_mx(
-                        out=acc[:],
+                        out=product[:],
                         lhsT=codes[:, first : first + P].bitcast(FP8X4),
                         lhsT_scale=scales[:, first : first + P],
                         rhs=w_codes[:].bitcast(FP8X4),
@@ -147,23 +162,23 @@ def tile_attributegnn_pb_t_kernel(tc, attr_rep, bwd_proj, self_weighted, out):
                         start=(g == 0),
                         stop=(g == PASSES - 1),
                     )
-                proj[(u, m)] = acc
+                proj[(u, v)] = product
 
         def relu(u):
             if u % 2 == 0:
                 relu_out[u // 2] = relu_pool.tile([P, 2 * UNIT_TILES, N], F32, name="relu_out")
-            r = relu_out[u // 2]
-            for m in range(UNIT_TILES):
-                nc.scalar.activation(out=r[:, UNIT_TILES * (u % 2) + m, :], in_=proj[(u, m)][:], func=ACT.Relu)
+            pair = relu_out[u // 2]
+            for v in range(UNIT_TILES):
+                nc.scalar.activation(out=pair[:, UNIT_TILES * (u % 2) + v, :], in_=proj[(u, v)][:], func=ACT.Relu)
 
-        def add_in(a, r, rows, so_far=None):
+        def add_in(a, relu_part, rows, so_far=None):
             if a == 0:
-                nc.vector.tensor_scalar_mul(out=total[:, rows, :], in0=r, scalar1=weight[:, 0:1])
+                nc.vector.tensor_scalar_mul(out=total[:, rows, :], in0=relu_part, scalar1=gain[:, 0:1])
             else:
                 nc.vector.scalar_tensor_tensor(
                     out=total[:, rows, :],
-                    in0=r,
-                    scalar=weight[:, a : a + 1],
+                    in0=relu_part,
+                    scalar=gain[:, a : a + 1],
                     in1=total[:, rows, :] if so_far is None else so_far,
                     op0=ALU.mult,
                     op1=ALU.add,
@@ -173,7 +188,7 @@ def tile_attributegnn_pb_t_kernel(tc, attr_rep, bwd_proj, self_weighted, out):
             nc.tensor.matmul(
                 out=tile0_sum[:],
                 lhsT=diag[:, a, :],
-                rhs=relu_out[2 * a][:, 0, :],
+                rhs=relu_out[a * UNITS_PER_TYPE // 2][:, 0, :],
                 start=(a == 0),
                 stop=(a == TYPES - 2),
             )
@@ -184,48 +199,17 @@ def tile_attributegnn_pb_t_kernel(tc, attr_rep, bwd_proj, self_weighted, out):
                 if u % 2 == 1:
                     skip = 1 if quarter == 1 else 0
                     first = UNIT_TILES * (quarter - 1)
-                    add_in(a, relu_out[u // 2][:, skip : 2 * UNIT_TILES, :], slice(first + skip, first + 2 * UNIT_TILES))
+                    rows = slice(first + skip, first + 2 * UNIT_TILES)
+                    add_in(a, relu_out[u // 2][:, skip : 2 * UNIT_TILES, :], rows)
             else:
-                for m in range(UNIT_TILES):
-                    row = UNIT_TILES * quarter + m
-                    add_in(a, relu_out[u // 2][:, UNIT_TILES * (u % 2) + m, :], row, tile0_sum[:] if row == 0 else None)
-                    nc.sync.dma_start(out=out_view[:, row, :], in_=total[:, row, :])
+                for v in range(UNIT_TILES):
+                    m = UNIT_TILES * quarter + v
+                    add_in(a, relu_out[u // 2][:, UNIT_TILES * (u % 2) + v, :], m, tile0_sum[:] if m == 0 else None)
+                    nc.sync.dma_start(out=out_view[:, m, :], in_=total[:, m, :])
 
-        loads = [("w", (0, 0)), ("x", 0), ("w", (0, 1)), ("x", 1), ("w", (1, 0)), ("x", 2), ("x", 3), ("w", (1, 1))]
-        for a in range(1, TYPES):
-            loads.append(("x", 4 * a))
-            loads.append(("x", 4 * a + 1))
-            if a + 1 < TYPES:
-                loads.append(("w", (a + 1, 0)))
-            loads.append(("x", 4 * a + 2))
-            loads.append(("x", 4 * a + 3))
-            if a + 1 < TYPES:
-                loads.append(("w", (a + 1, 1)))
-        issued = [0]
-
-        def issue_loads(last_unit):
-            while issued[0] < len(loads):
-                kind, what = loads[issued[0]]
-                if kind == "x" and what > last_unit:
-                    break
-                if kind == "x":
-                    load_x(what)
-                else:
-                    load_w(what[0], what[1])
-                issued[0] += 1
-
-        w_steps = []
-        for a in range(1, TYPES):
-            for g in range(PASSES):
-                w_steps.append((regroup_w, a, g))
-                w_steps.append((quantise_w, a, g))
-
-        def w_step(j):
-            if 0 <= j < len(w_steps):
-                step, a, g = w_steps[j]
-                step(a, g)
-
-        issue_loads(LEAD + AHEAD - 1)
+        load_w(0, 0)
+        for u in range(LEAD + AHEAD):
+            load_unit(u)
         regroup_w(0, 0)
         transposes(0)
         evacuate(0)
@@ -233,10 +217,11 @@ def tile_attributegnn_pb_t_kernel(tc, attr_rep, bwd_proj, self_weighted, out):
         regroup_w(0, 1)
         quantise_x(0)
         quantise_w(0, 1)
+
         transposed = 1
-        w_done = 0
         for i in range(UNITS):
-            issue_loads(i + LEAD + AHEAD)
+            if i + LEAD + AHEAD < UNITS:
+                load_unit(i + LEAD + AHEAD)
             lead = 1 if i < SHORT_LEAD_UNITS else LEAD
             while transposed <= min(UNITS - 1, i + lead):
                 transposes(transposed)
@@ -248,9 +233,9 @@ def tile_attributegnn_pb_t_kernel(tc, attr_rep, bwd_proj, self_weighted, out):
                 accumulate_tile0(i // UNITS_PER_TYPE)
             if i + 1 < UNITS:
                 quantise_x(i + 1)
-            while w_done <= i + 1:
-                w_step(w_done)
-                w_done += 1
+            if i == 0:
+                weight_step(0)
+            weight_step(i + 1)
             if i >= 1:
                 accumulate(i - 1)
         accumulate(UNITS - 1)

@@ -26,6 +26,8 @@ LEAD = 2
 SHORT_LEAD_UNITS = 3
 AHEAD = 8
 SCALAR_COLS = (160, 0, 0, 0, 0, 64, 96, 64)
+WARM_BEFORE = 6
+WARM_BETWEEN = 5
 
 
 def tile_attributegnn_pb_t_kernel(tc, attr_rep, bwd_proj, self_weighted, out):
@@ -70,6 +72,14 @@ def tile_attributegnn_pb_t_kernel(tc, attr_rep, bwd_proj, self_weighted, out):
         warm_in = const.tile([P, 1], F32, name="warm_in")
         warm_out = const.tile([P, 1], F32, name="warm_out")
         nc.vector.memset(warm_in[:], 0.0)
+        zeros = const.tile([P, N], BF16, name="zeros")
+        nc.vector.memset(zeros[:], 0.0)
+
+        def warm_up(count):
+            for step in range(count):
+                idle = psum_mm.tile([P, N], F32, name="proj")
+                nc.tensor.matmul(out=idle[:], lhsT=zeros[:, 0:P], rhs=zeros[:], start=True, stop=True)
+
         nc.scalar.activation(out=warm_out[:], in_=warm_in[:], func=ACT.Relu)
 
         def load_w(a, g):
@@ -211,7 +221,9 @@ def tile_attributegnn_pb_t_kernel(tc, attr_rep, bwd_proj, self_weighted, out):
         for u in range(LEAD + AHEAD):
             load_unit(u)
         regroup_w(0, 0)
+        warm_up(WARM_BEFORE)
         transposes(0)
+        warm_up(WARM_BETWEEN)
         evacuate(0)
         quantise_w(0, 0)
         regroup_w(0, 1)

@@ -26,6 +26,7 @@ LEAD = 2
 SHORT_LEAD_UNITS = 3
 AHEAD = 8
 SCALAR_COLS = (160, 0, 0, 0, 0, 64, 96, 64)
+SUM_COLS = N // UNITS_PER_TYPE
 WARM_BEFORE = 6
 WARM_BETWEEN = 5
 
@@ -194,13 +195,14 @@ def tile_attributegnn_pb_t_kernel(tc, attr_rep, bwd_proj, self_weighted, out):
                     op1=ALU.add,
                 )
 
-        def accumulate_tile0(a):
+        def accumulate_tile0(a, piece):
+            cols = slice(piece * SUM_COLS, (piece + 1) * SUM_COLS)
             nc.tensor.matmul(
-                out=tile0_sum[:],
+                out=tile0_sum[:, cols],
                 lhsT=diag[:, a, :],
-                rhs=relu_out[a * UNITS_PER_TYPE // 2][:, 0, :],
-                start=(a == 0),
-                stop=(a == TYPES - 2),
+                rhs=relu_out[a * UNITS_PER_TYPE // 2][:, 0, cols],
+                start=(a == 0 and piece == 0),
+                stop=(a == TYPES - 2 and piece == UNITS_PER_TYPE - 1),
             )
 
         def accumulate(u):
@@ -241,8 +243,8 @@ def tile_attributegnn_pb_t_kernel(tc, attr_rep, bwd_proj, self_weighted, out):
                 transposed += 1
             multiply(i)
             relu(i)
-            if i % UNITS_PER_TYPE == 1 and i // UNITS_PER_TYPE < TYPES - 1:
-                accumulate_tile0(i // UNITS_PER_TYPE)
+            if 1 <= i <= UNITS_PER_TYPE * (TYPES - 1):
+                accumulate_tile0((i - 1) // UNITS_PER_TYPE, (i - 1) % UNITS_PER_TYPE)
             if i + 1 < UNITS:
                 quantise_x(i + 1)
             if i == 0:

@@ -25,7 +25,7 @@ WORDS = K // 2
 LEAD = 2
 SHORT_LEAD_UNITS = 3
 AHEAD = 8
-SCALAR_COLS = (160, 0, 0, 0, 0, 64, 96, 64)
+SCALAR_COLS = (160, 0, 0, 0, 0, 0, 32, 32)
 SUM_COLS = N // UNITS_PER_TYPE
 WARM_BEFORE = 6
 WARM_BETWEEN = 5
@@ -46,7 +46,7 @@ def tile_attributegnn_pb_t_kernel(tc, attr_rep, bwd_proj, self_weighted, out):
         wgrp_pool = ctx.enter_context(tc.tile_pool(name="wgrp", bufs=2))
         wq_pool = ctx.enter_context(tc.tile_pool(name="wq", bufs=2 * PASSES))
         relu_pool = ctx.enter_context(tc.tile_pool(name="relu", bufs=3))
-        psum_t = ctx.enter_context(tc.psum_pool(name="psum_t", bufs=2 * UNIT_TILES))
+        psum_t = ctx.enter_context(tc.psum_pool(name="psum_t", bufs=3))
         psum_mm = ctx.enter_context(tc.psum_pool(name="psum_mm", bufs=3))
         psum_sum = ctx.enter_context(tc.psum_pool(name="psum_sum", bufs=1))
         ctx.enter_context(tc.manual_schedule())
@@ -69,6 +69,7 @@ def tile_attributegnn_pb_t_kernel(tc, attr_rep, bwd_proj, self_weighted, out):
                 out=diag[:, a, :], in0=ident[:], scalar1=gain[:, a : a + 1], scalar2=0.0, op0=ALU.mult, op1=ALU.add
             )
         tile0_sum = psum_sum.tile([P, N], F32, name="tile0_sum")
+        tile1_sum = psum_sum.tile([P, N], F32, name="tile1_sum")
         total = const.tile([P, NODE_TILES, N], F32, name="total")
         warm_in = const.tile([P, 1], F32, name="warm_in")
         warm_out = const.tile([P, 1], F32, name="warm_out")
@@ -204,19 +205,26 @@ def tile_attributegnn_pb_t_kernel(tc, attr_rep, bwd_proj, self_weighted, out):
                 start=(a == 0 and piece == 0),
                 stop=(a == TYPES - 2 and piece == UNITS_PER_TYPE - 1),
             )
+            nc.tensor.matmul(
+                out=tile1_sum[:, cols],
+                lhsT=diag[:, a, :],
+                rhs=relu_out[a * UNITS_PER_TYPE // 2][:, 1, cols],
+                start=(a == 0 and piece == 0),
+                stop=(a == TYPES - 2 and piece == UNITS_PER_TYPE - 1),
+            )
 
         def accumulate(u):
             a, quarter = divmod(u, UNITS_PER_TYPE)
             if a < TYPES - 1:
                 if u % 2 == 1:
-                    skip = 1 if quarter == 1 else 0
+                    skip = 2 if quarter == 1 else 0
                     first = UNIT_TILES * (quarter - 1)
                     rows = slice(first + skip, first + 2 * UNIT_TILES)
                     add_in(a, relu_out[u // 2][:, skip : 2 * UNIT_TILES, :], rows)
             else:
                 for v in range(UNIT_TILES):
                     m = UNIT_TILES * quarter + v
-                    add_in(a, relu_out[u // 2][:, UNIT_TILES * (u % 2) + v, :], m, tile0_sum[:] if m == 0 else None)
+                    add_in(a, relu_out[u // 2][:, UNIT_TILES * (u % 2) + v, :], m, tile0_sum[:] if m == 0 else (tile1_sum[:] if m == 1 else None))
                     nc.sync.dma_start(out=out_view[:, m, :], in_=total[:, m, :])
 
         load_w(0, 0)

@@ -26,6 +26,9 @@ LEAD = 2
 SHORT_LEAD_UNITS = 3
 AHEAD = 8
 SCALAR_COLS = (160, 0, 0, 0, 0, 0, 32, 32)
+SUM_TILES = 2
+T_BANKS = 3
+MM_BANKS = 3
 SUM_COLS = N // UNITS_PER_TYPE
 WARM_BEFORE = 6
 WARM_BETWEEN = 5
@@ -46,8 +49,8 @@ def tile_attributegnn_pb_t_kernel(tc, attr_rep, bwd_proj, self_weighted, out):
         wgrp_pool = ctx.enter_context(tc.tile_pool(name="wgrp", bufs=2))
         wq_pool = ctx.enter_context(tc.tile_pool(name="wq", bufs=2 * PASSES))
         relu_pool = ctx.enter_context(tc.tile_pool(name="relu", bufs=3))
-        psum_t = ctx.enter_context(tc.psum_pool(name="psum_t", bufs=3))
-        psum_mm = ctx.enter_context(tc.psum_pool(name="psum_mm", bufs=3))
+        psum_t = ctx.enter_context(tc.psum_pool(name="psum_t", bufs=T_BANKS))
+        psum_mm = ctx.enter_context(tc.psum_pool(name="psum_mm", bufs=MM_BANKS))
         psum_sum = ctx.enter_context(tc.psum_pool(name="psum_sum", bufs=1))
         ctx.enter_context(tc.manual_schedule())
 
@@ -68,8 +71,7 @@ def tile_attributegnn_pb_t_kernel(tc, attr_rep, bwd_proj, self_weighted, out):
             nc.gpsimd.tensor_scalar(
                 out=diag[:, a, :], in0=ident[:], scalar1=gain[:, a : a + 1], scalar2=0.0, op0=ALU.mult, op1=ALU.add
             )
-        tile0_sum = psum_sum.tile([P, N], F32, name="tile0_sum")
-        tile1_sum = psum_sum.tile([P, N], F32, name="tile1_sum")
+        tile_sum = [psum_sum.tile([P, N], F32, name="tile_sum%d" % m) for m in range(SUM_TILES)]
         total = const.tile([P, NODE_TILES, N], F32, name="total")
         warm_in = const.tile([P, 1], F32, name="warm_in")
         warm_out = const.tile([P, 1], F32, name="warm_out")
@@ -196,19 +198,12 @@ def tile_attributegnn_pb_t_kernel(tc, attr_rep, bwd_proj, self_weighted, out):
                     op1=ALU.add,
                 )
 
-        def accumulate_tile0(a, piece):
+        def sum_on_tensor(m, a, piece):
             cols = slice(piece * SUM_COLS, (piece + 1) * SUM_COLS)
             nc.tensor.matmul(
-                out=tile0_sum[:, cols],
+                out=tile_sum[m][:, cols],
                 lhsT=diag[:, a, :],
-                rhs=relu_out[a * UNITS_PER_TYPE // 2][:, 0, cols],
-                start=(a == 0 and piece == 0),
-                stop=(a == TYPES - 2 and piece == UNITS_PER_TYPE - 1),
-            )
-            nc.tensor.matmul(
-                out=tile1_sum[:, cols],
-                lhsT=diag[:, a, :],
-                rhs=relu_out[a * UNITS_PER_TYPE // 2][:, 1, cols],
+                rhs=relu_out[a * UNITS_PER_TYPE // 2][:, m, cols],
                 start=(a == 0 and piece == 0),
                 stop=(a == TYPES - 2 and piece == UNITS_PER_TYPE - 1),
             )
@@ -217,14 +212,14 @@ def tile_attributegnn_pb_t_kernel(tc, attr_rep, bwd_proj, self_weighted, out):
             a, quarter = divmod(u, UNITS_PER_TYPE)
             if a < TYPES - 1:
                 if u % 2 == 1:
-                    skip = 2 if quarter == 1 else 0
+                    skip = SUM_TILES if quarter == 1 else 0
                     first = UNIT_TILES * (quarter - 1)
                     rows = slice(first + skip, first + 2 * UNIT_TILES)
                     add_in(a, relu_out[u // 2][:, skip : 2 * UNIT_TILES, :], rows)
             else:
                 for v in range(UNIT_TILES):
                     m = UNIT_TILES * quarter + v
-                    add_in(a, relu_out[u // 2][:, UNIT_TILES * (u % 2) + v, :], m, tile0_sum[:] if m == 0 else (tile1_sum[:] if m == 1 else None))
+                    add_in(a, relu_out[u // 2][:, UNIT_TILES * (u % 2) + v, :], m, tile_sum[m][:] if m < SUM_TILES else None)
                     nc.sync.dma_start(out=out_view[:, m, :], in_=total[:, m, :])
 
         load_w(0, 0)
@@ -249,10 +244,14 @@ def tile_attributegnn_pb_t_kernel(tc, attr_rep, bwd_proj, self_weighted, out):
                 transposes(transposed)
                 evacuate(transposed)
                 transposed += 1
+            step = i - 1
+            summing = 0 <= step < UNITS_PER_TYPE * (TYPES - 1)
+            if summing:
+                sum_on_tensor(0, step // UNITS_PER_TYPE, step % UNITS_PER_TYPE)
             multiply(i)
             relu(i)
-            if 1 <= i <= UNITS_PER_TYPE * (TYPES - 1):
-                accumulate_tile0((i - 1) // UNITS_PER_TYPE, (i - 1) % UNITS_PER_TYPE)
+            if summing:
+                sum_on_tensor(1, step // UNITS_PER_TYPE, step % UNITS_PER_TYPE)
             if i + 1 < UNITS:
                 quantise_x(i + 1)
             if i == 0:

@@ -60,17 +60,23 @@ def tile_attributegnn_pb_t_kernel(tc, attr_rep, bwd_proj, self_weighted, out):
 
         ident = const.tile([P, P], F32, name="ident")
         make_identity(nc, ident[:])
-        gain_bf = const.tile([P, TYPES], BF16, name="gain_bf")
-        nc.scalar.dma_start(
-            out=gain_bf[:], in_=self_weighted.rearrange("o a i -> (o a i)").partition_broadcast(P)
-        )
+        gain_row = const.tile([P, TYPES], BF16, name="gain_row")
+        nc.vector.memset(gain_row[:], 0.0)
+        nc.scalar.dma_start(out=gain_row[0:1, :], in_=self_weighted.rearrange("o a i -> o (a i)"))
+        ones = const.tile([P, P], BF16, name="ones")
+        nc.vector.memset(ones[:], 1.0)
         gain = const.tile([P, TYPES], F32, name="gain")
-        nc.gpsimd.tensor_copy(out=gain[:], in_=gain_bf[:])
         diag = const.tile([P, TYPES - 1, P], F32, name="diag")
-        for a in range(TYPES - 1):
-            nc.gpsimd.tensor_scalar(
-                out=diag[:, a, :], in0=ident[:], scalar1=gain[:, a : a + 1], scalar2=0.0, op0=ALU.mult, op1=ALU.add
-            )
+
+        def spread_gains():
+            spread = psum_mm.tile([P, N], F32, name="proj")
+            nc.tensor.matmul(out=spread[:, 0:TYPES], lhsT=ones[:], rhs=gain_row[:], start=True, stop=True)
+            nc.vector.tensor_copy(out=gain[:], in_=spread[:, 0:TYPES])
+            for a in range(TYPES - 1):
+                nc.gpsimd.tensor_scalar(
+                    out=diag[:, a, :], in0=ident[:], scalar1=gain[:, a : a + 1], scalar2=0.0, op0=ALU.mult, op1=ALU.add
+                )
+
         tile_sum = [psum_sum.tile([P, N], F32, name="tile_sum%d" % m) for m in range(SUM_TILES)]
         total = const.tile([P, NODE_TILES, N], F32, name="total")
         warm_in = const.tile([P, 1], F32, name="warm_in")
@@ -227,6 +233,7 @@ def tile_attributegnn_pb_t_kernel(tc, attr_rep, bwd_proj, self_weighted, out):
             load_unit(u)
         regroup_w(0, 0)
         warm_up(WARM_BEFORE)
+        spread_gains()
         transposes(0)
         warm_up(WARM_BETWEEN)
         evacuate(0)

from contextlib import ExitStack

import concourse.mybir as mybir
from concourse.masks import make_identity

BF16 = mybir.dt.bfloat16
F32 = mybir.dt.float32
U32 = mybir.dt.uint32
U8 = mybir.dt.uint8
FP8X4 = mybir.dt.float8_e4m3fn_x4
ALU = mybir.AluOpType
ACT = mybir.ActivationFunctionType

P = 128
NODES, TYPES, K, N = 1024, 8, 1024, 512
FLOPS = 2 * NODES * TYPES * K * N
PACK = 4
PASSES = K // (P * PACK)
NODE_TILES = NODES // P
UNIT_TILES = 2
UNITS_PER_TYPE = NODE_TILES // UNIT_TILES
UNITS = TYPES * UNITS_PER_TYPE
WORDS = K // 2

LEAD = 2
SHORT_LEAD_UNITS = 3
AHEAD = 8
SCALAR_COLS = (160, 0, 0, 0, 0, 0, 32, 32)
SUM_TILES = 2
T_BANKS = 3
MM_BANKS = 3
SUM_COLS = N // UNITS_PER_TYPE
WARM_BEFORE = 6
WARM_BETWEEN = 5


def tile_attributegnn_pb_t_kernel(tc, attr_rep, bwd_proj, self_weighted, out):
    nc = tc.nc
    x_view = attr_rep.rearrange("(r m) a k -> r m a k", m=NODE_TILES)
    w_view = bwd_proj.rearrange("a (g h q e) n -> a g q h e n", g=PASSES, h=2, q=P, e=2)
    out_view = out.rearrange("(r m) n -> r m n", m=NODE_TILES)

    with ExitStack() as ctx:
        const = ctx.enter_context(tc.tile_pool(name="const", bufs=1))
        xraw_pool = ctx.enter_context(tc.tile_pool(name="xraw", bufs=LEAD + AHEAD + 2))
        wraw_pool = ctx.enter_context(tc.tile_pool(name="wraw", bufs=8))
        xgrp_pool = ctx.enter_context(tc.tile_pool(name="xgrp", bufs=3))
        xq_pool = ctx.enter_context(tc.tile_pool(name="xq", bufs=3))
        wgrp_pool = ctx.enter_context(tc.tile_pool(name="wgrp", bufs=2))
        wq_pool = ctx.enter_context(tc.tile_pool(name="wq", bufs=2 * PASSES))
        relu_pool = ctx.enter_context(tc.tile_pool(name="relu", bufs=3))
        psum_t = ctx.enter_context(tc.psum_pool(name="psum_t", bufs=T_BANKS))
        psum_mm = ctx.enter_context(tc.psum_pool(name="psum_mm", bufs=MM_BANKS))
        psum_sum = ctx.enter_context(tc.psum_pool(name="psum_sum", bufs=1))
        ctx.enter_context(tc.manual_schedule())

        x_raw, x_t, x_grp, x_q = {}, {}, {}, {}
        w_raw, w_grp, w_q = {}, {}, {}
        proj, relu_out = {}, {}

        ident = const.tile([P, P], F32, name="ident")
        make_identity(nc, ident[:])
        gain_row = const.tile([P, TYPES], BF16, name="gain_row")
        nc.vector.memset(gain_row[:], 0.0)
        nc.scalar.dma_start(out=gain_row[0:1, :], in_=self_weighted.rearrange("o a i -> o (a i)"))
        ones = const.tile([P, P], BF16, name="ones")
        nc.vector.memset(ones[:], 1.0)
        gain = const.tile([P, TYPES], F32, name="gain")
        diag = const.tile([P, TYPES - 1, P], F32, name="diag")

        def spread_gains():
            spread = psum_mm.tile([P, N], F32, name="proj")
            nc.tensor.matmul(out=spread[:, 0:TYPES], lhsT=ones[:], rhs=gain_row[:], start=True, stop=True)
            nc.vector.tensor_copy(out=gain[:], in_=spread[:, 0:TYPES])
            for a in range(TYPES - 1):
                nc.gpsimd.tensor_scalar(
                    out=diag[:, a, :], in0=ident[:], scalar1=gain[:, a : a + 1], scalar2=0.0, op0=ALU.mult, op1=ALU.add
                )

        tile_sum = [psum_sum.tile([P, N], F32, name="tile_sum%d" % m) for m in range(SUM_TILES)]
        total = const.tile([P, NODE_TILES, N], F32, name="total")
        warm_in = const.tile([P, 1], F32, name="warm_in")
        warm_out = const.tile([P, 1], F32, name="warm_out")
        nc.vector.memset(warm_in[:], 0.0)
        zeros = const.tile([P, N], BF16, name="zeros")
        nc.vector.memset(zeros[:], 0.0)

        def warm_up(count):
            for step in range(count):
                idle = psum_mm.tile([P, N], F32, name="proj")
                nc.tensor.matmul(out=idle[:], lhsT=zeros[:, 0:P], rhs=zeros[:], start=True, stop=True)

        nc.scalar.activation(out=warm_out[:], in_=warm_in[:], func=ACT.Relu)

        def load_w(a, g):
            raw = wraw_pool.tile([P, PACK, N], BF16, name="w_raw")
            nc.sync.dma_start(out=raw[:].rearrange("q (h e) n -> q h e n", h=2), in_=w_view[a, g])
            w_raw[(a, g)] = raw

        def load_unit(u):
            a, quarter = divmod(u, UNITS_PER_TYPE)
            raw = xraw_pool.tile([P, UNIT_TILES * K], BF16, name="x_raw")
            nc.sync.dma_start(
                out=raw[:].rearrange("p (v k) -> p v k", v=UNIT_TILES),
                in_=x_view[:, UNIT_TILES * quarter : UNIT_TILES * (quarter + 1), a, :],
            )
            x_raw[u] = raw
            if u == 0:
                load_w(0, 1)
            elif u % 2 == 1 and (u + 3) // UNITS_PER_TYPE < TYPES:
                load_w((u + 3) // UNITS_PER_TYPE, ((u + 3) % UNITS_PER_TYPE) // 2)

        def transposes(u):
            words = x_raw[u][:].bitcast(F32)
            for v in range(UNIT_TILES):
                bank = psum_t.tile([P, 2 * PASSES, P], F32, name="x_t")
                for s in range(2 * PASSES):
                    first = v * WORDS + s * P
                    nc.tensor.transpose(bank[:, s, :], words[:, first : first + P], ident[:])
                x_t[(u, v)] = bank

        def evacuate(u):
            grp = xgrp_pool.tile([P, UNIT_TILES * K], BF16, name="x_grp", align_bytes=64)
            words = grp[:].bitcast(F32)
            for v in range(UNIT_TILES):
                nc.scalar.copy(
                    out=words[:, v * WORDS : (v + 1) * WORDS].rearrange("p (g r h) -> p g r h", g=PASSES, h=2),
                    in_=x_t[(u, v)][:].rearrange("p (g h) r -> p g r h", h=2),
                )
            x_grp[u] = grp

        def quantise_x(u):
            codes = xq_pool.tile([P, UNIT_TILES * PASSES * P], U32, name="x_codes", align_bytes=64)
            scales = xq_pool.tile([P, UNIT_TILES * PASSES * P], U8, name="x_scales", align_bytes=64)
            nc.vector.quantize_mx(out=codes[:].bitcast(FP8X4), scales=scales[:], in_=x_grp[u][:])
            x_q[u] = (codes, scales)

        def regroup_w(a, g):
            grp = wgrp_pool.tile([P, N, PACK], BF16, name="w_grp", align_bytes=64)
            cut = N - SCALAR_COLS[a]
            nc.vector.tensor_copy(
                out=grp[:, 0:cut, :].rearrange("p (c d) t -> p c t d", d=4),
                in_=w_raw[(a, g)][:, :, 0:cut].rearrange("p t (c d) -> p c t d", d=4),
            )
            if cut < N:
                nc.scalar.copy(
                    out=grp[:, cut:N, :].rearrange("p (c d) t -> p c t d", d=4),
                    in_=w_raw[(a, g)][:, :, cut:N].rearrange("p t (c d) -> p c t d", d=4),
                )
            w_grp[(a, g)] = grp

        def quantise_w(a, g):
            codes = wq_pool.tile([P, N], U32, name="w_codes", align_bytes=64)
            scales = wq_pool.tile([P, N], U8, name="w_scales", align_bytes=64)
            nc.vector.quantize_mx(
                out=codes[:].bitcast(FP8X4), scales=scales[:], in_=w_grp[(a, g)][:].rearrange("p n t -> p (n t)")
            )
            w_q[(a, g)] = (codes, scales)

        def weight_step(step):
            a, g = 1 + step // (2 * PASSES), (step // 2) % PASSES
            if a < TYPES:
                if step % 2 == 0:
                    regroup_w(a, g)
                else:
                    quantise_w(a, g)

        def multiply(u):
            a = u // UNITS_PER_TYPE
            codes, scales = x_q[u]
            for v in range(UNIT_TILES):
                product = psum_mm.tile([P, N], F32, name="proj")
                for g in range(PASSES):
                    first = (PASSES * v + g) * P
                    w_codes, w_scales = w_q[(a, g)]
                    nc.tensor.matmul_mx(
                        out=product[:],
                        lhsT=codes[:, first : first + P].bitcast(FP8X4),
                        lhsT_scale=scales[:, first : first + P],
                        rhs=w_codes[:].bitcast(FP8X4),
                        rhs_scale=w_scales[:],
                        start=(g == 0),
                        stop=(g == PASSES - 1),
                    )
                proj[(u, v)] = product

        def relu(u):
            if u % 2 == 0:
                relu_out[u // 2] = relu_pool.tile([P, 2 * UNIT_TILES, N], F32, name="relu_out")
            pair = relu_out[u // 2]
            for v in range(UNIT_TILES):
                nc.scalar.activation(out=pair[:, UNIT_TILES * (u % 2) + v, :], in_=proj[(u, v)][:], func=ACT.Relu)

        def add_in(a, relu_part, rows, so_far=None):
            if a == 0:
                nc.vector.tensor_scalar_mul(out=total[:, rows, :], in0=relu_part, scalar1=gain[:, 0:1])
            else:
                nc.vector.scalar_tensor_tensor(
                    out=total[:, rows, :],
                    in0=relu_part,
                    scalar=gain[:, a : a + 1],
                    in1=total[:, rows, :] if so_far is None else so_far,
                    op0=ALU.mult,
                    op1=ALU.add,
                )

        def sum_on_tensor(m, a, piece):
            cols = slice(piece * SUM_COLS, (piece + 1) * SUM_COLS)
            nc.tensor.matmul(
                out=tile_sum[m][:, cols],
                lhsT=diag[:, a, :],
                rhs=relu_out[a * UNITS_PER_TYPE // 2][:, m, cols],
                start=(a == 0 and piece == 0),
                stop=(a == TYPES - 2 and piece == UNITS_PER_TYPE - 1),
            )

        def accumulate(u):
            a, quarter = divmod(u, UNITS_PER_TYPE)
            if a < TYPES - 1:
                if u % 2 == 1:
                    skip = SUM_TILES if quarter == 1 else 0
                    first = UNIT_TILES * (quarter - 1)
                    rows = slice(first + skip, first + 2 * UNIT_TILES)
                    add_in(a, relu_out[u // 2][:, skip : 2 * UNIT_TILES, :], rows)
            else:
                for v in range(UNIT_TILES):
                    m = UNIT_TILES * quarter + v
                    add_in(a, relu_out[u // 2][:, UNIT_TILES * (u % 2) + v, :], m, tile_sum[m][:] if m < SUM_TILES else None)
                    nc.sync.dma_start(out=out_view[:, m, :], in_=total[:, m, :])

        load_w(0, 0)
        for u in range(LEAD + AHEAD):
            load_unit(u)
        regroup_w(0, 0)
        warm_up(WARM_BEFORE)
        spread_gains()
        transposes(0)
        warm_up(WARM_BETWEEN)
        evacuate(0)
        quantise_w(0, 0)
        regroup_w(0, 1)
        quantise_x(0)
        quantise_w(0, 1)

        transposed = 1
        for i in range(UNITS):
            if i + LEAD + AHEAD < UNITS:
                load_unit(i + LEAD + AHEAD)
            lead = 1 if i < SHORT_LEAD_UNITS else LEAD
            while transposed <= min(UNITS - 1, i + lead):
                transposes(transposed)
                evacuate(transposed)
                transposed += 1
            step = i - 1
            summing = 0 <= step < UNITS_PER_TYPE * (TYPES - 1)
            if summing:
                sum_on_tensor(0, step // UNITS_PER_TYPE, step % UNITS_PER_TYPE)
            multiply(i)
            relu(i)
            if summing:
                sum_on_tensor(1, step // UNITS_PER_TYPE, step % UNITS_PER_TYPE)
            if i + 1 < UNITS:
                quantise_x(i + 1)
            if i == 0:
                weight_step(0)
            weight_step(i + 1)
            if i >= 1:
                accumulate(i - 1)
        accumulate(UNITS - 1)
